import numpy as np
import ml_dtypes


def mxq(x, axis, fmt="e4m3"):
    dtype, down = {"e4m3": (ml_dtypes.float8_e4m3fn, 7), "e5m2": (ml_dtypes.float8_e5m2, 14)}[fmt]
    v = np.moveaxis(np.asarray(x, np.float32).astype(ml_dtypes.bfloat16).astype(np.float64), axis, -1)
    blocks = v.reshape(v.shape[:-1] + (-1, 32))
    amax = np.abs(blocks).max(-1, keepdims=True)
    byte = np.maximum(np.where(amax > 0, np.frexp(amax)[1] - 1 + 127, 0) - down, 1)
    scale = np.exp2(byte - 127.0)
    codes = (blocks / scale).astype(np.float32).astype(dtype).astype(np.float64)
    return np.moveaxis((codes * scale).reshape(v.shape), -1, axis)


WIDE = False


def mx_kscale(k):
    if not WIDE:
        return np.ones(k)
    levels = np.array([30, -30])
    if k % 512:
        return np.exp2(np.random.permutation(np.resize(levels, k // 32))).repeat(32)
    a = np.empty((k // 512, 16))
    for p in range(k // 512):
        a[p, :8] = np.random.permutation(np.resize(levels, 8))
        for g in range(8):
            far = levels[np.abs(levels - a[p, g]) >= 10]
            a[p, g + 8] = far[np.random.randint(len(far))]
    return np.exp2(a.ravel()).repeat(32)


BF16 = ml_dtypes.bfloat16


def bf(x):
    return np.asarray(x, np.float32).astype(BF16)


def f64(x):
    return np.asarray(x).astype(np.float64)


E2M1 = np.array([0.0, 0.5, 1.0, 1.5, 2.0, 3.0, 4.0, 6.0, -0.0, -0.5, -1.0, -1.5, -2.0, -3.0, -4.0, -6.0])


def pack_weight(w, fmt):
    k, n = w.shape
    w = f64(bf(w)).reshape(k // 32, 32, n)
    amax = np.abs(w).max(1)
    if fmt == "e4m3":
        byte = np.frexp(amax)[1] - 1 + 127 - 7
    else:
        mant, ex = np.frexp(amax / 6.0)
        byte = np.where(mant > 0.5, ex, ex - 1) + 127
    byte = np.clip(np.where(amax > 0, byte, 1), 1, 254)
    scaled = (w * np.exp2(127.0 - byte)[:, None, :]).reshape(k, n).astype(np.float32)
    by_word = np.ascontiguousarray(scaled.reshape(k // 512, 128, 4, n).transpose(0, 1, 3, 2))
    if fmt == "e4m3":
        words = by_word.astype(ml_dtypes.float8_e4m3fn).view(np.uint8)
    else:
        c = by_word.astype(ml_dtypes.float4_e2m1fn).view(np.uint8) & 0xF
        words = c[..., 0::2] | (c[..., 1::2] << 4)
    return np.ascontiguousarray(words), np.ascontiguousarray(byte.astype(np.uint8).reshape(k // 512, 16, n))


def unpack_weight(words, scales, fmt):
    g, p, n, _ = words.shape
    if fmt == "e4m3":
        vals = np.ascontiguousarray(words).view(ml_dtypes.float8_e4m3fn).astype(np.float64)
    else:
        nib = np.empty((g, p, n, 4), np.uint8)
        nib[..., 0::2] = words & 0xF
        nib[..., 1::2] = words >> 4
        vals = E2M1[nib]
    vals = vals * np.repeat(np.exp2(scales.astype(np.float64) - 127.0), 8, axis=1)[..., None]
    return vals.transpose(0, 1, 3, 2).reshape(g * 512, n)

def pack4(w):
    words, scales = pack_weight(w, "e2m1")
    return words.reshape(words.shape[0], 128, -1), scales


def unpack4(words, scales):
    return unpack_weight(words.reshape(words.shape[0], 128, -1, 2), scales, "e2m1")


B, S, DIM, H, NKV, HD, GS = 1, 512, 2048, 16, 4, 128, 128
QS = H * HD
KVS = NKV * HD
HALF = HD // 2
ROPE_BASE = 10000.0
RMS_EPS = 1.1920929e-07


def rms_norm(v):
    return v / np.sqrt(np.mean(v * v, axis=-1, keepdims=True) + RMS_EPS)


def rope_cos_sin():
    inv_freq = 1.0 / ROPE_BASE ** (np.arange(0, HD, 2) / HD)
    freqs = np.outer(np.arange(S), inv_freq)
    return np.cos(freqs)[None, :, None, :], np.sin(freqs)[None, :, None, :]


def apply_rotary_emb(u, cos, sin):
    u1, u2 = u[..., :HALF], u[..., HALF:]
    return np.concatenate((u1 * cos + u2 * sin, u1 * -sin + u2 * cos), axis=-1)


def setup_inputs():
    s = mx_kscale(DIM)
    x = bf(np.random.standard_normal((B, S, DIM)) * s)
    w = np.random.standard_normal((QS + 2 * KVS, DIM)) * 0.66 / np.sqrt(DIM) / s[None, :]
    words, scales = pack4(np.ascontiguousarray(w.T))
    q_gain = bf(1.0 + 0.1 * np.random.standard_normal(H))
    return {"x": x,
            "w_qkv_tern_words": words,
            "w_qkv_tern_scales": scales,
            "q_gain": q_gain}


def reference(x, w_qkv_tern_words, w_qkv_tern_scales, q_gain):
    qkv = mxq(f64(x), 2, "e5m2") @ unpack4(w_qkv_tern_words, w_qkv_tern_scales)
    q = qkv[..., :QS].reshape(B, S, H, HD)
    k = qkv[..., QS:QS + KVS].reshape(B, S, NKV, HD)
    v = qkv[..., QS + KVS:].reshape(B, S, NKV, HD)
    q, k = rms_norm(q), rms_norm(k)
    cos, sin = rope_cos_sin()
    q = apply_rotary_emb(q, cos, sin)
    k = apply_rotary_emb(k, cos, sin)
    q = q * f64(q_gain)[None, None, :, None]
    return q, k, v

@@ -1,0 +1,236 @@
+from contextlib import ExitStack
+
+import concourse.mybir as mybir
+from concourse.masks import make_identity
+
+S, DIM, H, NKV, HD = 512, 2048, 16, 4, 128
+HALF = HD // 2
+NCOLS = (H + 2 * NKV) * HD
+FLOPS = 2 * S * DIM * NCOLS
+ROPE_BASE = 10000.0
+RMS_EPS_F32 = 2.0 ** -23
+TWO_PI = 6.283185307179586
+
+F32 = mybir.dt.float32
+BF16 = mybir.dt.bfloat16
+I32 = mybir.dt.int32
+U32 = mybir.dt.uint32
+U8 = mybir.dt.uint8
+E5M2X4 = mybir.dt.float8_e5m2_x4
+E2M1X4 = mybir.dt.float4_e2m1fn_x4
+ACT = mybir.ActivationFunctionType
+ALU = mybir.AluOpType
+
+P = 128
+NT = S // P
+NG = DIM // 512
+NJ = NCOLS // 512
+K_GROUP = 4
+V_GROUP = 5
+HPG = 4
+
+
+def tile_causalselfattention_pa_kernel(tc, x, w_words, w_scales, q_gain, out_0, out_1, out_2):
+    nc = tc.nc
+    x2d = x.flatten_outer_dims()
+    outs = [
+        out_0.rearrange("b t h d -> (b t) (h d)"),
+        out_1.rearrange("b t h d -> (b t) (h d)"),
+        out_2.rearrange("b t h d -> (b t) (h d)"),
+    ]
+
+    with ExitStack() as ctx:
+        keep = ctx.enter_context(tc.tile_pool(name="keep", bufs=1))
+        small = ctx.enter_context(tc.tile_pool(name="small", bufs=4))
+        work = ctx.enter_context(tc.tile_pool(name="work", bufs=4))
+        outp = ctx.enter_context(tc.tile_pool(name="outp", bufs=8))
+        psum = ctx.enter_context(tc.psum_pool(name="psum", bufs=8))
+        ctx.enter_context(tc.manual_schedule())
+
+        x_sb = [keep.tile([P, DIM], BF16, name="x_sb%d" % a, align_bytes=64) for a in range(NT)]
+        grouped = [keep.tile([P, DIM], BF16, name="grouped%d" % a, align_bytes=64) for a in range(NT)]
+        x_codes = [keep.tile([P, DIM // 4], U32, name="x_codes%d" % a, align_bytes=64) for a in range(NT)]
+        x_scales = [keep.tile([P, DIM // 4], U8, name="x_scales%d" % a, align_bytes=64) for a in range(NT)]
+        w_sb = [keep.tile([P, NG, 1024], U8, name="w_sb%d" % j, align_bytes=64) for j in range(NJ)]
+        w_plane = [keep.tile([P, NG, 512], U8, name="w_plane%d" % j, align_bytes=64) for j in range(NJ)]
+
+        def load_x(a, pieces):
+            width = DIM // pieces
+            for c in range(pieces):
+                nc.sync.dma_start(
+                    out=x_sb[a][:, width * c : width * (c + 1)], in_=x2d[P * a : P * (a + 1), width * c : width * (c + 1)]
+                )
+
+        def load_w(j):
+            nc.sync.dma_start(
+                out=w_sb[j][:].bitcast(I32),
+                in_=w_words[:, :, 1024 * j : 1024 * (j + 1)].rearrange("g p n -> p g n").bitcast(I32),
+            )
+
+        def load_w_scales(j):
+            for quad in range(4):
+                nc.sync.dma_start(
+                    out=w_plane[j][32 * quad : 32 * quad + 4, :, :].bitcast(I32),
+                    in_=w_scales[:, 4 * quad : 4 * quad + 4, 512 * j : 512 * (j + 1)]
+                    .rearrange("g r n -> r g n")
+                    .bitcast(I32),
+                )
+
+        gain = keep.tile([P, H], BF16, name="gain")
+        nc.scalar.dma_start(out=gain[:], in_=q_gain.partition_broadcast(P))
+
+        eps_t = keep.tile([P, 1], F32, name="eps_t")
+        nc.vector.memset(eps_t[:], RMS_EPS_F32)
+        warm = keep.tile([P, 2], F32, name="warm")
+        nc.scalar.activation(out=warm[:, 0:1], in_=eps_t[:], func=ACT.Sin)
+
+        tpos = keep.tile([P, NT], F32, name="tpos")
+        nc.gpsimd.iota(tpos[:], pattern=[[P, NT]], base=0, channel_multiplier=1, allow_small_or_imprecise_dtypes=True)
+        nc.gpsimd.memset(w_plane[0][:].bitcast(F32), 0.0)
+        ident = keep.tile([P, P], F32, name="ident")
+        make_identity(nc, ident[:])
+        for j in range(1, NJ):
+            nc.gpsimd.memset(w_plane[j][:].bitcast(F32), 0.0)
+
+        load_x(0, 2)
+        load_w_scales(0)
+        load_x(1, 1)
+        load_w(0)
+        load_w_scales(1)
+        load_w_scales(2)
+        load_w(1)
+        load_x(2, 1)
+        load_w(2)
+        load_x(3, 1)
+        for j in range(3, NJ):
+            load_w_scales(j)
+        for j in range(3, NJ):
+            load_w(j)
+
+        ratio = ROPE_BASE ** (-1.0 / HALF)
+        turns = keep.tile([P, NT, HALF], F32, name="turns")
+        for d0 in range(8):
+            nc.vector.tensor_scalar_mul(out=turns[:, :, d0], in0=tpos[:], scalar1=ratio ** d0 / TWO_PI)
+        for d1 in range(1, 8):
+            nc.vector.tensor_scalar_mul(
+                out=turns[:, :, 8 * d1 : 8 * d1 + 8], in0=turns[:, :, 0:8], scalar1=ratio ** (8 * d1)
+            )
+        whole_i = keep.tile([P, NT, HALF], I32, name="whole_i")
+        nc.vector.tensor_copy(out=whole_i[:], in_=turns[:])
+        whole_f = keep.tile([P, NT, HALF], F32, name="whole_f")
+        nc.vector.tensor_copy(out=whole_f[:], in_=whole_i[:])
+        frac = keep.tile([P, NT, 2, HALF], F32, name="frac")
+        nc.vector.tensor_tensor(out=frac[:, :, 1, :], in0=turns[:], in1=whole_f[:], op=ALU.subtract)
+        nc.vector.tensor_scalar_add(out=frac[:, :, 0, :], in0=frac[:, :, 1, :], scalar1=0.25)
+        neg_turn = keep.tile([P, NT, 2, HALF], F32, name="neg_turn")
+        frac_flat = frac[:].rearrange("p a b d -> p (a b d)")
+        nc.vector.scalar_tensor_tensor(
+            out=neg_turn[:].rearrange("p a b d -> p (a b d)"),
+            in0=frac_flat, scalar=0.5, in1=frac_flat, op0=ALU.is_gt, op1=ALU.subtract,
+        )
+        tab = keep.tile([P, NT, 4, HALF], F32, name="tab")
+        nc.scalar.activation(out=tab[:, :, 0:2, :], in_=neg_turn[:], func=ACT.Sin, scale=-TWO_PI)
+        nc.scalar.activation(out=tab[:, :, 2, :], in_=neg_turn[:, :, 1, :], func=ACT.Sin, scale=TWO_PI)
+        nc.scalar.activation(out=tab[:, :, 3, :], in_=neg_turn[:, :, 0, :], func=ACT.Sin, scale=-TWO_PI)
+        nc.scalar.activation(out=warm[:, 1:2], in_=eps_t[:], func=ACT.Abs_reciprocal_sqrt)
+
+        def prepare_x(a, engine_copy):
+            words = x_sb[a][:].bitcast(F32)
+            for b in range(2):
+                xt = psum.tile([P, 512], F32, tag="bank")
+                for gg in range(2):
+                    g = 2 * b + gg
+                    for u in range(2):
+                        nc.tensor.transpose(
+                            xt[:, (2 * gg + u) * P : (2 * gg + u + 1) * P],
+                            words[:, 256 * g + u : 256 * (g + 1) : 2],
+                            ident[:],
+                        )
+                engine_copy(
+                    out=grouped[a][:, 1024 * b : 1024 * (b + 1)].bitcast(F32).rearrange("p (g r u) -> p g r u", g=2, u=2),
+                    in_=xt[:].rearrange("p (g u r) -> p g r u", g=2, u=2),
+                )
+            nc.vector.quantize_mx(out=x_codes[a][:].bitcast(E5M2X4), scales=x_scales[a][:], in_=grouped[a][:])
+
+        def mx_unit(a, j):
+            acc = psum.tile([P, 512], F32, tag="bank")
+            for g in range(NG):
+                nc.tensor.matmul_mx(
+                    out=acc[:],
+                    lhsT=x_codes[a][:, P * g : P * (g + 1)].bitcast(E5M2X4),
+                    lhsT_scale=x_scales[a][:, P * g : P * (g + 1)],
+                    rhs=w_sb[j][:, g, :].bitcast(E2M1X4),
+                    rhs_scale=w_plane[j][:, g, :],
+                    start=(g == 0),
+                    stop=(g == NG - 1),
+                )
+            return acc
+
+        def store(a, j, o):
+            which, col = (0, 512 * j) if j < K_GROUP else (j - K_GROUP + 1, 0)
+            nc.sync.dma_start(out=outs[which][P * a : P * (a + 1), col : col + 512], in_=o[:])
+
+        def rope_head(pend, h):
+            nc.vector.scalar_tensor_tensor(
+                out=pend["ab"][:, 2 * HD * h : 2 * HD * (h + 1)].rearrange("p (r d) -> p r d", r=2),
+                in0=pend["acc"][:, HD * h : HD * (h + 1)].unsqueeze(1).to_broadcast([P, 2, HD]),
+                scalar=pend["rg"][:, h : h + 1],
+                in1=tab[:, pend["a"], :, :].rearrange("p (r c) d -> p r (c d)", r=2),
+                op0=ALU.mult,
+                op1=ALU.mult,
+            )
+
+        def finish(pend):
+            o = outp.tile([P, 512], F32, tag="o")
+            pairs = pend["ab"][:].rearrange("p (m two d) -> p m two d", two=2, d=HALF)
+            adder = nc.vector if pend["late"] else nc.gpsimd
+            adder.tensor_tensor(
+                out=o[:].rearrange("p (m d) -> p m d", d=HALF), in0=pairs[:, :, 0, :], in1=pairs[:, :, 1, :], op=ALU.add
+            )
+            store(pend["a"], pend["j"], o)
+
+        def flush(pending, first):
+            for pend in pending:
+                for h in range(first, HPG):
+                    rope_head(pend, h)
+                finish(pend)
+            pending.clear()
+
+        program = [("x", 0), ("x", 1), (0, 0), (1, 0), (0, 1), (1, 1), ("x", 2), (0, 2), (1, 2), ("x", 3)]
+        program += [(2, 0), (2, 1), (2, 2), (3, 0), (3, 1), (3, 2)]
+        program += [(a, j) for j in (3, 4, 5) for a in range(NT)]
+        n_rope = NT * V_GROUP
+        done = 0
+        pending = []
+        for a, j in program:
+            if a == "x":
+                flush(pending, 0)
+                prepare_x(j, nc.vector.tensor_copy if j < 2 else nc.scalar.copy)
+                continue
+            acc = mx_unit(a, j)
+            if j == V_GROUP:
+                flush(pending, 0)
+                o = outp.tile([P, 512], F32, tag="o")
+                nc.scalar.copy(out=o[:], in_=acc[:])
+                store(a, j, o)
+                continue
+            ss = small.tile([P, HPG], F32, tag="ss")
+            for h in range(HPG):
+                junk = work.tile([P, HD], F32, tag="junk")
+                nc.scalar.activation(
+                    out=junk[:], in_=acc[:, HD * h : HD * (h + 1)], func=ACT.Square,
+                    scale=HD ** -0.5, accum_out=ss[:, h : h + 1],
+                )
+            rg = small.tile([P, HPG], F32, tag="rs")
+            nc.scalar.activation(out=rg[:], in_=ss[:], func=ACT.Abs_reciprocal_sqrt, bias=eps_t[:], scale=1.0)
+            for pend in pending:
+                for h in range(HPG - 1):
+                    rope_head(pend, h)
+            if j < K_GROUP:
+                rs = rg
+                rg = small.tile([P, HPG], F32, tag="rg")
+                nc.vector.tensor_tensor(out=rg[:], in0=rs[:], in1=gain[:, HPG * j : HPG * (j + 1)], op=ALU.mult)
+            flush(pending, HPG - 1)
+            ab = work.tile([P, 2 * 512], F32, tag="ab")
+            done += 1
+            pending.append({"acc": acc, "rg": rg, "a": a, "j": j, "ab": ab, "late": done > n_rope - 2})

@@ -84,6 +84,7 @@ def tile_causalselfattention_pa_kernel(tc, x, w_words, w_scales, q_gain, out_0, 
         warm = keep.tile([P, 2], F32, name="warm")
         nc.scalar.activation(out=warm[:, 0:1], in_=eps_t[:], func=ACT.Sin)
 
+        gain32 = keep.tile([P, H], F32, name="gain32")
         tpos = keep.tile([P, NT], F32, name="tpos")
         nc.gpsimd.iota(tpos[:], pattern=[[P, NT]], base=0, channel_multiplier=1, allow_small_or_imprecise_dtypes=True)
         nc.gpsimd.memset(w_plane[0][:].bitcast(F32), 0.0)
@@ -128,6 +129,7 @@ def tile_causalselfattention_pa_kernel(tc, x, w_words, w_scales, q_gain, out_0, 
             out=neg_turn[:].rearrange("p a b d -> p (a b d)"),
             in0=frac_flat, scalar=0.5, in1=frac_flat, op0=ALU.is_gt, op1=ALU.subtract,
         )
+        nc.vector.tensor_copy(out=gain32[:], in_=gain[:])
         tab = keep.tile([P, NT, 4, HALF], F32, name="tab")
         nc.scalar.activation(out=tab[:, :, 0:2, :], in_=neg_turn[:], func=ACT.Sin, scale=-TWO_PI)
         nc.scalar.activation(out=tab[:, :, 2, :], in_=neg_turn[:, :, 1, :], func=ACT.Sin, scale=TWO_PI)
@@ -223,14 +225,15 @@ def tile_causalselfattention_pa_kernel(tc, x, w_words, w_scales, q_gain, out_0, 
                 )
             rg = small.tile([P, HPG], F32, tag="rs")
             nc.scalar.activation(out=rg[:], in_=ss[:], func=ACT.Abs_reciprocal_sqrt, bias=eps_t[:], scale=1.0)
-            for pend in pending:
-                for h in range(HPG - 1):
-                    rope_head(pend, h)
             if j < K_GROUP:
                 rs = rg
                 rg = small.tile([P, HPG], F32, tag="rg")
-                nc.vector.tensor_tensor(out=rg[:], in0=rs[:], in1=gain[:, HPG * j : HPG * (j + 1)], op=ALU.mult)
-            flush(pending, HPG - 1)
+                for h in range(HPG):
+                    nc.scalar.activation(
+                        out=rg[:, h : h + 1], in_=rs[:, h : h + 1], func=ACT.Copy,
+                        scale=gain32[:, HPG * j + h : HPG * j + h + 1],
+                    )
+            flush(pending, 0)
             ab = work.tile([P, 2 * 512], F32, tag="ab")
             done += 1
             pending.append({"acc": acc, "rg": rg, "a": a, "j": j, "ab": ab, "late": done > n_rope - 2})

@@ -41,9 +41,9 @@ def tile_causalselfattention_pa_kernel(tc, x, w_words, w_scales, q_gain, out_0, 
 
     with ExitStack() as ctx:
         keep = ctx.enter_context(tc.tile_pool(name="keep", bufs=1))
-        small = ctx.enter_context(tc.tile_pool(name="small", bufs=4))
-        work = ctx.enter_context(tc.tile_pool(name="work", bufs=4))
-        outp = ctx.enter_context(tc.tile_pool(name="outp", bufs=8))
+        small = ctx.enter_context(tc.tile_pool(name="small", bufs=6))
+        work = ctx.enter_context(tc.tile_pool(name="work", bufs=6))
+        outp = ctx.enter_context(tc.tile_pool(name="outp", bufs=NT * NJ))
         psum = ctx.enter_context(tc.psum_pool(name="psum", bufs=8))
         ctx.enter_context(tc.manual_schedule())
 
@@ -61,11 +61,13 @@ def tile_causalselfattention_pa_kernel(tc, x, w_words, w_scales, q_gain, out_0, 
                     out=x_sb[a][:, width * c : width * (c + 1)], in_=x2d[P * a : P * (a + 1), width * c : width * (c + 1)]
                 )
 
-        def load_w(j):
-            nc.sync.dma_start(
-                out=w_sb[j][:].bitcast(I32),
-                in_=w_words[:, :, 1024 * j : 1024 * (j + 1)].rearrange("g p n -> p g n").bitcast(I32),
-            )
+        def load_w(j, pieces):
+            n_g = NG // pieces
+            for c in range(pieces):
+                nc.sync.dma_start(
+                    out=w_sb[j][:, n_g * c : n_g * (c + 1), :].bitcast(I32),
+                    in_=w_words[n_g * c : n_g * (c + 1), :, 1024 * j : 1024 * (j + 1)].rearrange("g p n -> p g n").bitcast(I32),
+                )
 
         def load_w_scales(j):
             for quad in range(4):
@@ -76,37 +78,38 @@ def tile_causalselfattention_pa_kernel(tc, x, w_words, w_scales, q_gain, out_0, 
                     .bitcast(I32),
                 )
 
-        gain = keep.tile([P, H], BF16, name="gain")
-        nc.scalar.dma_start(out=gain[:], in_=q_gain.partition_broadcast(P))
-
         eps_t = keep.tile([P, 1], F32, name="eps_t")
         nc.vector.memset(eps_t[:], RMS_EPS_F32)
         warm = keep.tile([P, 2], F32, name="warm")
         nc.scalar.activation(out=warm[:, 0:1], in_=eps_t[:], func=ACT.Sin)
 
-        gain32 = keep.tile([P, H], F32, name="gain32")
         tpos = keep.tile([P, NT], F32, name="tpos")
         nc.gpsimd.iota(tpos[:], pattern=[[P, NT]], base=0, channel_multiplier=1, allow_small_or_imprecise_dtypes=True)
-        nc.gpsimd.memset(w_plane[0][:].bitcast(F32), 0.0)
         ident = keep.tile([P, P], F32, name="ident")
         make_identity(nc, ident[:])
-        for j in range(1, NJ):
-            nc.gpsimd.memset(w_plane[j][:].bitcast(F32), 0.0)
+
+        gain_row = keep.tile([P, H], BF16, name="gain_row")
+        nc.vector.memset(gain_row[:], 0.0)
+        nc.vector.memset(w_plane[0][:].bitcast(I32), 0)
+        ones = keep.tile([P, P], BF16, name="ones")
+        nc.vector.memset(ones[:], 1.0)
+        gain32 = keep.tile([P, H], F32, name="gain32")
 
         load_x(0, 2)
+        nc.sync.dma_start(out=gain_row[0:1, :], in_=q_gain.unsqueeze(0))
         load_w_scales(0)
+        load_w(0, 2)
         load_x(1, 1)
-        load_w(0)
-        load_w_scales(1)
-        load_w_scales(2)
-        load_w(1)
         load_x(2, 1)
-        load_w(2)
         load_x(3, 1)
-        for j in range(3, NJ):
-            load_w_scales(j)
-        for j in range(3, NJ):
-            load_w(j)
+
+        idle = psum.tile([P, 512], F32, tag="bank")
+
+        def idle_matmuls(n):
+            for i in range(n):
+                nc.tensor.matmul(idle[:, 0:P], lhsT=ident[:], rhs=ident[:], start=True, stop=True)
+
+        idle_matmuls(4)
 
         ratio = ROPE_BASE ** (-1.0 / HALF)
         turns = keep.tile([P, NT, HALF], F32, name="turns")
@@ -129,15 +132,18 @@ def tile_causalselfattention_pa_kernel(tc, x, w_words, w_scales, q_gain, out_0, 
             out=neg_turn[:].rearrange("p a b d -> p (a b d)"),
             in0=frac_flat, scalar=0.5, in1=frac_flat, op0=ALU.is_gt, op1=ALU.subtract,
         )
-        nc.vector.tensor_copy(out=gain32[:], in_=gain[:])
         tab = keep.tile([P, NT, 4, HALF], F32, name="tab")
-        nc.scalar.activation(out=tab[:, :, 0:2, :], in_=neg_turn[:], func=ACT.Sin, scale=-TWO_PI)
-        nc.scalar.activation(out=tab[:, :, 2, :], in_=neg_turn[:, :, 1, :], func=ACT.Sin, scale=TWO_PI)
-        nc.scalar.activation(out=tab[:, :, 3, :], in_=neg_turn[:, :, 0, :], func=ACT.Sin, scale=-TWO_PI)
-        nc.scalar.activation(out=warm[:, 1:2], in_=eps_t[:], func=ACT.Abs_reciprocal_sqrt)
 
-        def prepare_x(a, engine_copy):
+        def scalar_tables():
+            nc.scalar.activation(out=tab[:, :, 0:2, :], in_=neg_turn[:], func=ACT.Sin, scale=-TWO_PI)
+            nc.scalar.activation(out=tab[:, :, 2, :], in_=neg_turn[:, :, 1, :], func=ACT.Sin, scale=TWO_PI)
+            nc.scalar.activation(out=tab[:, :, 3, :], in_=neg_turn[:, :, 0, :], func=ACT.Sin, scale=-TWO_PI)
+            nc.scalar.copy(out=gain32[:], in_=idle[:, P : P + H])
+            nc.scalar.activation(out=warm[:, 1:2], in_=eps_t[:], func=ACT.Abs_reciprocal_sqrt)
+
+        def transpose_x(a):
             words = x_sb[a][:].bitcast(F32)
+            banks = []
             for b in range(2):
                 xt = psum.tile([P, 512], F32, tag="bank")
                 for gg in range(2):
@@ -148,11 +154,24 @@ def tile_causalselfattention_pa_kernel(tc, x, w_words, w_scales, q_gain, out_0, 
                             words[:, 256 * g + u : 256 * (g + 1) : 2],
                             ident[:],
                         )
+                banks.append(xt)
+            return banks
+
+        def copy_x(a, banks, engine_copy):
+            for b in range(2):
                 engine_copy(
                     out=grouped[a][:, 1024 * b : 1024 * (b + 1)].bitcast(F32).rearrange("p (g r u) -> p g r u", g=2, u=2),
-                    in_=xt[:].rearrange("p (g u r) -> p g r u", g=2, u=2),
+                    in_=banks[b][:].rearrange("p (g u r) -> p g r u", g=2, u=2),
                 )
-            nc.vector.quantize_mx(out=x_codes[a][:].bitcast(E5M2X4), scales=x_scales[a][:], in_=grouped[a][:])
+
+        def quantize_x(a, pieces):
+            w = DIM // pieces
+            for c in range(pieces):
+                nc.vector.quantize_mx(
+                    out=x_codes[a][:, (w // 4) * c : (w // 4) * (c + 1)].bitcast(E5M2X4),
+                    scales=x_scales[a][:, (w // 4) * c : (w // 4) * (c + 1)],
+                    in_=grouped[a][:, w * c : w * (c + 1)],
+                )
 
         def mx_unit(a, j):
             acc = psum.tile([P, 512], F32, tag="bank")
@@ -191,31 +210,10 @@ def tile_causalselfattention_pa_kernel(tc, x, w_words, w_scales, q_gain, out_0, 
             )
             store(pend["a"], pend["j"], o)
 
-        def flush(pending, first):
-            for pend in pending:
-                for h in range(first, HPG):
-                    rope_head(pend, h)
-                finish(pend)
-            pending.clear()
-
-        program = [("x", 0), ("x", 1), (0, 0), (1, 0), (0, 1), (1, 1), ("x", 2), (0, 2), (1, 2), ("x", 3)]
-        program += [(2, 0), (2, 1), (2, 2), (3, 0), (3, 1), (3, 2)]
-        program += [(a, j) for j in (3, 4, 5) for a in range(NT)]
         n_rope = NT * V_GROUP
-        done = 0
-        pending = []
-        for a, j in program:
-            if a == "x":
-                flush(pending, 0)
-                prepare_x(j, nc.vector.tensor_copy if j < 2 else nc.scalar.copy)
-                continue
-            acc = mx_unit(a, j)
-            if j == V_GROUP:
-                flush(pending, 0)
-                o = outp.tile([P, 512], F32, tag="o")
-                nc.scalar.copy(out=o[:], in_=acc[:])
-                store(a, j, o)
-                continue
+        state = {"done": 0}
+
+        def norm_factors(a, j, acc):
             ss = small.tile([P, HPG], F32, tag="ss")
             for h in range(HPG):
                 junk = work.tile([P, HD], F32, tag="junk")
@@ -233,7 +231,60 @@ def tile_causalselfattention_pa_kernel(tc, x, w_words, w_scales, q_gain, out_0, 
                         out=rg[:, h : h + 1], in_=rs[:, h : h + 1], func=ACT.Copy,
                         scale=gain32[:, HPG * j + h : HPG * j + h + 1],
                     )
-            flush(pending, 0)
+            return rg
+
+        def rotate(a, j, acc, rg):
             ab = work.tile([P, 2 * 512], F32, tag="ab")
-            done += 1
-            pending.append({"acc": acc, "rg": rg, "a": a, "j": j, "ab": ab, "late": done > n_rope - 2})
+            state["done"] += 1
+            pend = {"acc": acc, "rg": rg, "a": a, "j": j, "ab": ab, "late": state["done"] > n_rope - 2}
+            for h in range(HPG):
+                rope_head(pend, h)
+            finish(pend)
+
+        def unit(a, j):
+            acc = mx_unit(a, j)
+            if j == V_GROUP:
+                o = outp.tile([P, 512], F32, tag="o")
+                nc.scalar.copy(out=o[:], in_=acc[:])
+                store(a, j, o)
+            else:
+                rotate(a, j, acc, norm_factors(a, j, acc))
+
+        xt0 = transpose_x(0)
+        idle_matmuls(2)
+        nc.tensor.matmul(idle[:, P : P + H], lhsT=ones[:], rhs=gain_row[:], start=True, stop=True)
+        copy_x(0, xt0, nc.scalar.copy)
+        quantize_x(0, 2)
+        scalar_tables()
+        for j in range(1, NJ):
+            nc.vector.memset(w_plane[j][:].bitcast(I32), 0)
+        load_w_scales(1)
+        load_w_scales(2)
+        load_w(1, 1)
+        load_w(2, 1)
+        for j in range(3, NJ):
+            load_w_scales(j)
+        for j in range(3, NJ):
+            load_w(j, 1)
+        acc00 = mx_unit(0, 0)
+        xt1 = transpose_x(1)
+        idle_matmuls(2)
+        copy_x(1, xt1, nc.vector.tensor_copy)
+        quantize_x(1, 1)
+        xt2 = transpose_x(2)
+        idle_matmuls(2)
+        rg00 = norm_factors(0, 0, acc00)
+        copy_x(2, xt2, nc.scalar.copy)
+        rotate(0, 0, acc00, rg00)
+        quantize_x(2, 1)
+        acc10 = mx_unit(1, 0)
+        rg10 = norm_factors(1, 0, acc10)
+        xt3 = transpose_x(3)
+        copy_x(3, xt3, nc.scalar.copy)
+        rotate(1, 0, acc10, rg10)
+        quantize_x(3, 1)
+        for a, j in [(2, 0), (0, 1), (1, 1), (2, 1), (3, 0), (3, 1)]:
+            unit(a, j)
+        for j in range(2, NJ):
+            for a in range(NT):
+                unit(a, j)

@@ -43,7 +43,7 @@ def tile_causalselfattention_pa_kernel(tc, x, w_words, w_scales, q_gain, out_0, 
         keep = ctx.enter_context(tc.tile_pool(name="keep", bufs=1))
         small = ctx.enter_context(tc.tile_pool(name="small", bufs=6))
         work = ctx.enter_context(tc.tile_pool(name="work", bufs=6))
-        outp = ctx.enter_context(tc.tile_pool(name="outp", bufs=NT * NJ))
+        outp = ctx.enter_context(tc.tile_pool(name="outp", bufs=NT * NJ + 2))
         psum = ctx.enter_context(tc.psum_pool(name="psum", bufs=8))
         ctx.enter_context(tc.manual_schedule())
 
@@ -187,10 +187,6 @@ def tile_causalselfattention_pa_kernel(tc, x, w_words, w_scales, q_gain, out_0, 
                 )
             return acc
 
-        def store(a, j, o):
-            which, col = (0, 512 * j) if j < K_GROUP else (j - K_GROUP + 1, 0)
-            nc.sync.dma_start(out=outs[which][P * a : P * (a + 1), col : col + 512], in_=o[:])
-
         def rope_head(pend, h):
             nc.vector.scalar_tensor_tensor(
                 out=pend["ab"][:, 2 * HD * h : 2 * HD * (h + 1)].rearrange("p (r d) -> p r d", r=2),
@@ -201,14 +197,20 @@ def tile_causalselfattention_pa_kernel(tc, x, w_words, w_scales, q_gain, out_0, 
                 op1=ALU.mult,
             )
 
-        def finish(pend):
-            o = outp.tile([P, 512], F32, tag="o")
+        def finish(pend, pieces=1):
             pairs = pend["ab"][:].rearrange("p (m two d) -> p m two d", two=2, d=HALF)
             adder = nc.vector if pend["late"] else nc.gpsimd
-            adder.tensor_tensor(
-                out=o[:].rearrange("p (m d) -> p m d", d=HALF), in0=pairs[:, :, 0, :], in1=pairs[:, :, 1, :], op=ALU.add
-            )
-            store(pend["a"], pend["j"], o)
+            which, col = (0, 512 * pend["j"]) if pend["j"] < K_GROUP else (1, 0)
+            w = 512 // pieces
+            for c in range(pieces):
+                o = outp.tile([P, w], F32, tag="o")
+                m0, m1 = (w // HALF) * c, (w // HALF) * (c + 1)
+                adder.tensor_tensor(
+                    out=o[:].rearrange("p (m d) -> p m d", d=HALF), in0=pairs[:, m0:m1, 0, :], in1=pairs[:, m0:m1, 1, :], op=ALU.add
+                )
+                nc.sync.dma_start(
+                    out=outs[which][P * pend["a"] : P * (pend["a"] + 1), col + w * c : col + w * (c + 1)], in_=o[:]
+                )
 
         n_rope = NT * V_GROUP
         state = {"done": 0}
@@ -233,20 +235,33 @@ def tile_causalselfattention_pa_kernel(tc, x, w_words, w_scales, q_gain, out_0, 
                     )
             return rg
 
+        held = []
+
         def rotate(a, j, acc, rg):
             ab = work.tile([P, 2 * 512], F32, tag="ab")
             state["done"] += 1
             pend = {"acc": acc, "rg": rg, "a": a, "j": j, "ab": ab, "late": state["done"] > n_rope - 2}
             for h in range(HPG):
                 rope_head(pend, h)
-            finish(pend)
+                if h == 1 and held:
+                    finish(held[0])
+                    held.clear()
+            if state["done"] == n_rope - 1:
+                held.append(pend)
+            elif state["done"] == n_rope:
+                finish(pend, 2)
+            else:
+                finish(pend)
 
         def unit(a, j):
             acc = mx_unit(a, j)
             if j == V_GROUP:
-                o = outp.tile([P, 512], F32, tag="o")
-                nc.scalar.copy(out=o[:], in_=acc[:])
-                store(a, j, o)
+                pieces = 2 if a == NT - 1 else 1
+                w = 512 // pieces
+                for c in range(pieces):
+                    o = outp.tile([P, w], F32, tag="o")
+                    nc.scalar.copy(out=o[:], in_=acc[:, w * c : w * (c + 1)])
+                    nc.sync.dma_start(out=outs[2][P * a : P * (a + 1), w * c : w * (c + 1)], in_=o[:])
             else:
                 rotate(a, j, acc, norm_factors(a, j, acc))
 

@@ -202,7 +202,7 @@ def tile_causalselfattention_pa_kernel(tc, x, w_words, w_scales, q_gain, out_0, 
             adder = nc.vector if pend["late"] else nc.gpsimd
             which, col = (0, 512 * pend["j"]) if pend["j"] < K_GROUP else (1, 0)
             w = 512 // pieces
-            for c in range(pieces):
+            for c in reversed(range(pieces)):
                 o = outp.tile([P, w], F32, tag="o")
                 m0, m1 = (w // HALF) * c, (w // HALF) * (c + 1)
                 adder.tensor_tensor(
@@ -241,9 +241,9 @@ def tile_causalselfattention_pa_kernel(tc, x, w_words, w_scales, q_gain, out_0, 
             ab = work.tile([P, 2 * 512], F32, tag="ab")
             state["done"] += 1
             pend = {"acc": acc, "rg": rg, "a": a, "j": j, "ab": ab, "late": state["done"] > n_rope - 2}
-            for h in range(HPG):
+            for h in reversed(range(HPG)):
                 rope_head(pend, h)
-                if h == 1 and held:
+                if h == HPG - 2 and held:
                     finish(held[0])
                     held.clear()
             if state["done"] == n_rope - 1:

@@ -215,7 +215,7 @@ def tile_causalselfattention_pa_kernel(tc, x, w_words, w_scales, q_gain, out_0, 
         n_rope = NT * V_GROUP
         state = {"done": 0}
 
-        def norm_factors(a, j, acc):
+        def mean_squares(acc):
             ss = small.tile([P, HPG], F32, tag="ss")
             for h in range(HPG):
                 junk = work.tile([P, HD], F32, tag="junk")
@@ -223,17 +223,26 @@ def tile_causalselfattention_pa_kernel(tc, x, w_words, w_scales, q_gain, out_0, 
                     out=junk[:], in_=acc[:, HD * h : HD * (h + 1)], func=ACT.Square,
                     scale=HD ** -0.5, accum_out=ss[:, h : h + 1],
                 )
-            rg = small.tile([P, HPG], F32, tag="rs")
-            nc.scalar.activation(out=rg[:], in_=ss[:], func=ACT.Abs_reciprocal_sqrt, bias=eps_t[:], scale=1.0)
-            if j < K_GROUP:
-                rs = rg
-                rg = small.tile([P, HPG], F32, tag="rg")
-                for h in range(HPG):
-                    nc.scalar.activation(
-                        out=rg[:, h : h + 1], in_=rs[:, h : h + 1], func=ACT.Copy,
-                        scale=gain32[:, HPG * j + h : HPG * j + h + 1],
-                    )
+            return ss
+
+        def inverse_root(ss):
+            rs = small.tile([P, HPG], F32, tag="rs")
+            nc.scalar.activation(out=rs[:], in_=ss[:], func=ACT.Abs_reciprocal_sqrt, bias=eps_t[:], scale=1.0)
+            return rs
+
+        def times_gain(j, rs):
+            if j == K_GROUP:
+                return rs
+            rg = small.tile([P, HPG], F32, tag="rg")
+            for h in range(HPG):
+                nc.scalar.activation(
+                    out=rg[:, h : h + 1], in_=rs[:, h : h + 1], func=ACT.Copy,
+                    scale=gain32[:, HPG * j + h : HPG * j + h + 1],
+                )
             return rg
+
+        def norm_factors(a, j, acc):
+            return times_gain(j, inverse_root(mean_squares(acc)))
 
         held = []
 
@@ -253,9 +262,17 @@ def tile_causalselfattention_pa_kernel(tc, x, w_words, w_scales, q_gain, out_0, 
             else:
                 finish(pend)
 
+        waiting = []
+
+        def flush():
+            for a, j, acc, rs in waiting:
+                rotate(a, j, acc, times_gain(j, rs))
+            waiting.clear()
+
         def unit(a, j):
             acc = mx_unit(a, j)
             if j == V_GROUP:
+                flush()
                 pieces = 2 if a == NT - 1 else 1
                 w = 512 // pieces
                 for c in range(pieces):
@@ -263,7 +280,9 @@ def tile_causalselfattention_pa_kernel(tc, x, w_words, w_scales, q_gain, out_0, 
                     nc.scalar.copy(out=o[:], in_=acc[:, w * c : w * (c + 1)])
                     nc.sync.dma_start(out=outs[2][P * a : P * (a + 1), w * c : w * (c + 1)], in_=o[:])
             else:
-                rotate(a, j, acc, norm_factors(a, j, acc))
+                ss = mean_squares(acc)
+                flush()
+                waiting.append((a, j, acc, inverse_root(ss)))
 
         xt0 = transpose_x(0)
         idle_matmuls(2)

@@ -52,7 +52,10 @@ def tile_causalselfattention_pa_kernel(tc, x, w_words, w_scales, q_gain, out_0, 
         x_codes = [keep.tile([P, DIM // 4], U32, name="x_codes%d" % a, align_bytes=64) for a in range(NT)]
         x_scales = [keep.tile([P, DIM // 4], U8, name="x_scales%d" % a, align_bytes=64) for a in range(NT)]
         w_sb = [keep.tile([P, NG, 1024], U8, name="w_sb%d" % j, align_bytes=64) for j in range(NJ)]
-        w_plane = [keep.tile([P, NG, 512], U8, name="w_plane%d" % j, align_bytes=64) for j in range(NJ)]
+        plane_of = [0, 1, 2, 3, 3, 3]
+        first_of = [0, 1, 2, 3]
+        plane_n = [1, 1, 1, 3]
+        w_plane = [keep.tile([P, NG, 512 * plane_n[i]], U8, name="w_plane%d" % i, align_bytes=64) for i in range(4)]
 
         def load_x(a, pieces):
             width = DIM // pieces
@@ -69,11 +72,12 @@ def tile_causalselfattention_pa_kernel(tc, x, w_words, w_scales, q_gain, out_0, 
                     in_=w_words[n_g * c : n_g * (c + 1), :, 1024 * j : 1024 * (j + 1)].rearrange("g p n -> p g n").bitcast(I32),
                 )
 
-        def load_w_scales(j):
+        def load_w_scales(i):
+            n = 512 * plane_n[i]
             for quad in range(4):
                 nc.sync.dma_start(
-                    out=w_plane[j][32 * quad : 32 * quad + 4, :, :].bitcast(I32),
-                    in_=w_scales[:, 4 * quad : 4 * quad + 4, 512 * j : 512 * (j + 1)]
+                    out=w_plane[i][32 * quad : 32 * quad + 4, :, :].bitcast(I32),
+                    in_=w_scales[:, 4 * quad : 4 * quad + 4, 512 * first_of[i] : 512 * first_of[i] + n]
                     .rearrange("g r n -> r g n")
                     .bitcast(I32),
                 )
@@ -91,6 +95,7 @@ def tile_causalselfattention_pa_kernel(tc, x, w_words, w_scales, q_gain, out_0, 
         gain_row = keep.tile([P, H], BF16, name="gain_row")
         nc.vector.memset(gain_row[:], 0.0)
         nc.vector.memset(w_plane[0][:].bitcast(I32), 0)
+        nc.vector.memset(w_plane[1][:].bitcast(I32), 0)
         ones = keep.tile([P, P], BF16, name="ones")
         nc.vector.memset(ones[:], 1.0)
         gain32 = keep.tile([P, H], F32, name="gain32")
@@ -98,10 +103,11 @@ def tile_causalselfattention_pa_kernel(tc, x, w_words, w_scales, q_gain, out_0, 
         load_x(0, 2)
         nc.sync.dma_start(out=gain_row[0:1, :], in_=q_gain.unsqueeze(0))
         load_w_scales(0)
-        load_w(0, 2)
+        load_w(0, 1)
         load_x(1, 1)
+        load_w_scales(1)
+        load_w(1, 1)
         load_x(2, 1)
-        load_x(3, 1)
 
         idle = psum.tile([P, 512], F32, tag="bank")
 
@@ -112,34 +118,28 @@ def tile_causalselfattention_pa_kernel(tc, x, w_words, w_scales, q_gain, out_0, 
         idle_matmuls(4)
 
         ratio = ROPE_BASE ** (-1.0 / HALF)
-        turns = keep.tile([P, NT, HALF], F32, name="turns")
-        for d0 in range(8):
-            nc.vector.tensor_scalar_mul(out=turns[:, :, d0], in0=tpos[:], scalar1=ratio ** d0 / TWO_PI)
-        for d1 in range(1, 8):
-            nc.vector.tensor_scalar_mul(
-                out=turns[:, :, 8 * d1 : 8 * d1 + 8], in0=turns[:, :, 0:8], scalar1=ratio ** (8 * d1)
-            )
-        whole_i = keep.tile([P, NT, HALF], I32, name="whole_i")
-        nc.vector.tensor_copy(out=whole_i[:], in_=turns[:])
-        whole_f = keep.tile([P, NT, HALF], F32, name="whole_f")
-        nc.vector.tensor_copy(out=whole_f[:], in_=whole_i[:])
-        frac = keep.tile([P, NT, 2, HALF], F32, name="frac")
-        nc.vector.tensor_tensor(out=frac[:, :, 1, :], in0=turns[:], in1=whole_f[:], op=ALU.subtract)
-        nc.vector.tensor_scalar_add(out=frac[:, :, 0, :], in0=frac[:, :, 1, :], scalar1=0.25)
-        neg_turn = keep.tile([P, NT, 2, HALF], F32, name="neg_turn")
-        frac_flat = frac[:].rearrange("p a b d -> p (a b d)")
-        nc.vector.scalar_tensor_tensor(
-            out=neg_turn[:].rearrange("p a b d -> p (a b d)"),
-            in0=frac_flat, scalar=0.5, in1=frac_flat, op0=ALU.is_gt, op1=ALU.subtract,
-        )
+        turns = keep.tile([P, 2, HALF, NT], F32, name="turns")
+        for d in range(4):
+            nc.vector.tensor_scalar_mul(out=turns[:, 1, d, :], in0=tpos[:], scalar1=ratio ** d / TWO_PI)
+        for n in (4, 16):
+            for m in range(1, 4):
+                nc.vector.tensor_scalar_mul(
+                    out=turns[:, 1, n * m : n * (m + 1), :], in0=turns[:, 1, 0:n, :], scalar1=ratio ** (n * m)
+                )
+        nc.vector.tensor_scalar_add(out=turns[:, 0, :, :], in0=turns[:, 1, :, :], scalar1=0.25)
+        whole = keep.tile([P, 2, HALF, NT], I32, name="whole")
+        nc.vector.tensor_copy(out=whole[:], in_=turns[:])
+        frac = keep.tile([P, 2, HALF, NT], F32, name="frac")
+        nc.vector.tensor_tensor(out=frac[:], in0=turns[:], in1=whole[:], op=ALU.subtract)
         tab = keep.tile([P, NT, 4, HALF], F32, name="tab")
 
         def scalar_tables():
-            nc.scalar.activation(out=tab[:, :, 0:2, :], in_=neg_turn[:], func=ACT.Sin, scale=-TWO_PI)
-            nc.scalar.activation(out=tab[:, :, 2, :], in_=neg_turn[:, :, 1, :], func=ACT.Sin, scale=TWO_PI)
-            nc.scalar.activation(out=tab[:, :, 3, :], in_=neg_turn[:, :, 0, :], func=ACT.Sin, scale=-TWO_PI)
-            nc.scalar.copy(out=gain32[:], in_=idle[:, P : P + H])
+            part = frac[:].rearrange("p c d a -> p a c d")
+            nc.scalar.activation(out=tab[:, :, 0:2, :], in_=part, func=ACT.Sin, scale=TWO_PI)
+            nc.scalar.activation(out=tab[:, :, 2, :], in_=part[:, :, 1, :], func=ACT.Sin, scale=-TWO_PI)
+            nc.scalar.activation(out=tab[:, :, 3, :], in_=part[:, :, 0, :], func=ACT.Sin, scale=TWO_PI)
             nc.scalar.activation(out=warm[:, 1:2], in_=eps_t[:], func=ACT.Abs_reciprocal_sqrt)
+            nc.scalar.copy(out=gain32[:], in_=idle[:, P : P + H])
 
         def transpose_x(a):
             words = x_sb[a][:].bitcast(F32)
@@ -157,22 +157,6 @@ def tile_causalselfattention_pa_kernel(tc, x, w_words, w_scales, q_gain, out_0, 
                 banks.append(xt)
             return banks
 
-        def copy_x(a, banks, engine_copy):
-            for b in range(2):
-                engine_copy(
-                    out=grouped[a][:, 1024 * b : 1024 * (b + 1)].bitcast(F32).rearrange("p (g r u) -> p g r u", g=2, u=2),
-                    in_=banks[b][:].rearrange("p (g u r) -> p g r u", g=2, u=2),
-                )
-
-        def quantize_x(a, pieces):
-            w = DIM // pieces
-            for c in range(pieces):
-                nc.vector.quantize_mx(
-                    out=x_codes[a][:, (w // 4) * c : (w // 4) * (c + 1)].bitcast(E5M2X4),
-                    scales=x_scales[a][:, (w // 4) * c : (w // 4) * (c + 1)],
-                    in_=grouped[a][:, w * c : w * (c + 1)],
-                )
-
         def mx_unit(a, j):
             acc = psum.tile([P, 512], F32, tag="bank")
             for g in range(NG):
@@ -181,7 +165,7 @@ def tile_causalselfattention_pa_kernel(tc, x, w_words, w_scales, q_gain, out_0, 
                     lhsT=x_codes[a][:, P * g : P * (g + 1)].bitcast(E5M2X4),
                     lhsT_scale=x_scales[a][:, P * g : P * (g + 1)],
                     rhs=w_sb[j][:, g, :].bitcast(E2M1X4),
-                    rhs_scale=w_plane[j][:, g, :],
+                    rhs_scale=w_plane[plane_of[j]][:, g, 512 * (j - first_of[plane_of[j]]) : 512 * (j - first_of[plane_of[j]] + 1)],
                     start=(g == 0),
                     stop=(g == NG - 1),
                 )
@@ -269,56 +253,129 @@ def tile_causalselfattention_pa_kernel(tc, x, w_words, w_scales, q_gain, out_0, 
                 rotate(a, j, acc, times_gain(j, rs))
             waiting.clear()
 
-        def unit(a, j):
-            acc = mx_unit(a, j)
-            if j == V_GROUP:
-                flush()
-                pieces = 2 if a == NT - 1 else 1
-                w = 512 // pieces
-                for c in range(pieces):
-                    o = outp.tile([P, w], F32, tag="o")
-                    nc.scalar.copy(out=o[:], in_=acc[:, w * c : w * (c + 1)])
-                    nc.sync.dma_start(out=outs[2][P * a : P * (a + 1), w * c : w * (c + 1)], in_=o[:])
-            else:
-                ss = mean_squares(acc)
-                flush()
-                waiting.append((a, j, acc, inverse_root(ss)))
+        acc, sums, root, factor = {}, {}, {}, {}
 
-        xt0 = transpose_x(0)
+        def mm(a, j):
+            acc[a, j] = mx_unit(a, j)
+
+        def squares(a, j):
+            sums[a, j] = mean_squares(acc[a, j])
+
+        def roots(a, j):
+            root[a, j] = inverse_root(sums[a, j])
+
+        def gains(a, j):
+            factor[a, j] = times_gain(j, root[a, j])
+
+        def turn(a, j):
+            rotate(a, j, acc[a, j], factor[a, j])
+
+        def plain(a, j):
+            pieces = 2 if a == NT - 1 else 1
+            w = 512 // pieces
+            for c in range(pieces):
+                o = outp.tile([P, w], F32, tag="o")
+                nc.scalar.copy(out=o[:], in_=acc[a, j][:, w * c : w * (c + 1)])
+                nc.scalar.dma_start(out=outs[2][P * a : P * (a + 1), w * c : w * (c + 1)], in_=o[:])
+
+        xt = {}
+
+        def flip(a):
+            xt[a] = transpose_x(a)
+
+        def copy_half(a, b, engine_copy):
+            engine_copy(
+                out=grouped[a][:, 1024 * b : 1024 * (b + 1)].bitcast(F32).rearrange("p (g r u) -> p g r u", g=2, u=2),
+                in_=xt[a][b][:].rearrange("p (g u r) -> p g r u", g=2, u=2),
+            )
+
+        def quant(a, c, pieces):
+            w = DIM // pieces
+            nc.vector.quantize_mx(
+                out=x_codes[a][:, (w // 4) * c : (w // 4) * (c + 1)].bitcast(E5M2X4),
+                scales=x_scales[a][:, (w // 4) * c : (w // 4) * (c + 1)],
+                in_=grouped[a][:, w * c : w * (c + 1)],
+            )
+
+        vcopy, scopy = nc.vector.tensor_copy, nc.scalar.copy
+        flip(0)
         idle_matmuls(2)
         nc.tensor.matmul(idle[:, P : P + H], lhsT=ones[:], rhs=gain_row[:], start=True, stop=True)
-        copy_x(0, xt0, nc.scalar.copy)
-        quantize_x(0, 2)
+        copy_half(0, 0, vcopy)
+        copy_half(0, 1, vcopy)
+        quant(0, 0, 2)
+        quant(0, 1, 2)
         scalar_tables()
-        for j in range(1, NJ):
-            nc.vector.memset(w_plane[j][:].bitcast(I32), 0)
-        load_w_scales(1)
+        nc.vector.memset(w_plane[2][:].bitcast(I32), 0)
+        nc.vector.memset(w_plane[3][:].bitcast(I32), 0)
         load_w_scales(2)
-        load_w(1, 1)
         load_w(2, 1)
-        for j in range(3, NJ):
-            load_w_scales(j)
-        for j in range(3, NJ):
-            load_w(j, 1)
-        acc00 = mx_unit(0, 0)
-        xt1 = transpose_x(1)
-        idle_matmuls(2)
-        copy_x(1, xt1, nc.vector.tensor_copy)
-        quantize_x(1, 1)
-        xt2 = transpose_x(2)
-        idle_matmuls(2)
-        rg00 = norm_factors(0, 0, acc00)
-        copy_x(2, xt2, nc.scalar.copy)
-        rotate(0, 0, acc00, rg00)
-        quantize_x(2, 1)
-        acc10 = mx_unit(1, 0)
-        rg10 = norm_factors(1, 0, acc10)
-        xt3 = transpose_x(3)
-        copy_x(3, xt3, nc.scalar.copy)
-        rotate(1, 0, acc10, rg10)
-        quantize_x(3, 1)
-        for a, j in [(2, 0), (0, 1), (1, 1), (2, 1), (3, 0), (3, 1)]:
-            unit(a, j)
-        for j in range(2, NJ):
-            for a in range(NT):
-                unit(a, j)
+        load_x(3, 1)
+        load_w_scales(3)
+        load_w(3, 1)
+        load_w(4, 1)
+        load_w(5, 1)
+
+        mm(0, 0)
+        flip(1)
+        copy_half(1, 0, vcopy)
+        copy_half(1, 1, vcopy)
+        quant(1, 0, 1)
+        squares(0, 0)
+        roots(0, 0)
+        gains(0, 0)
+        turn(0, 0)
+        mm(0, 1)
+        squares(0, 1)
+        roots(0, 1)
+        gains(0, 1)
+        turn(0, 1)
+        mm(1, 0)
+        squares(1, 0)
+        roots(1, 0)
+        mm(1, 1)
+        squares(1, 1)
+        gains(1, 0)
+        turn(1, 0)
+        roots(1, 1)
+        flip(2)
+        copy_half(2, 0, scopy)
+        copy_half(2, 1, scopy)
+        mm(0, 2)
+        squares(0, 2)
+        gains(1, 1)
+        quant(2, 0, 1)
+        turn(1, 1)
+        roots(0, 2)
+        mm(1, 2)
+        squares(1, 2)
+        gains(0, 2)
+        turn(0, 2)
+        roots(1, 2)
+        mm(2, 0)
+        flip(3)
+        squares(2, 0)
+        gains(1, 2)
+        turn(1, 2)
+        roots(2, 0)
+        copy_half(3, 0, scopy)
+        copy_half(3, 1, scopy)
+        mm(2, 1)
+        squares(2, 1)
+        gains(2, 0)
+        quant(3, 0, 1)
+        turn(2, 0)
+        roots(2, 1)
+        before = (2, 1)
+        for u in [(2, 2), (3, 0), (3, 1), (3, 2)] + [(a, j) for j in range(3, NJ) for a in range(NT)]:
+            mm(*u)
+            if u[1] == V_GROUP:
+                plain(*u)
+                continue
+            squares(*u)
+            gains(*before)
+            turn(*before)
+            roots(*u)
+            before = u
+        gains(*before)
+        turn(*before)

@@ -74,11 +74,11 @@ def tile_causalselfattention_pa_kernel(tc, x, w_words, w_scales, q_gain, out_0, 
 
         def load_w_scales(i):
             n = 512 * plane_n[i]
-            for quad in range(4):
+            for r in range(4):
                 nc.sync.dma_start(
-                    out=w_plane[i][32 * quad : 32 * quad + 4, :, :].bitcast(I32),
-                    in_=w_scales[:, 4 * quad : 4 * quad + 4, 512 * first_of[i] : 512 * first_of[i] + n]
-                    .rearrange("g r n -> r g n")
+                    out=w_plane[i][r : P : 32, :, :].bitcast(I32),
+                    in_=w_scales[:, r : 16 : 4, 512 * first_of[i] : 512 * first_of[i] + n]
+                    .rearrange("g q n -> q g n")
                     .bitcast(I32),
                 )
 
@@ -93,21 +93,18 @@ def tile_causalselfattention_pa_kernel(tc, x, w_words, w_scales, q_gain, out_0, 
         make_identity(nc, ident[:])
 
         gain_row = keep.tile([P, H], BF16, name="gain_row")
-        nc.vector.memset(gain_row[:], 0.0)
-        nc.vector.memset(w_plane[0][:].bitcast(I32), 0)
-        nc.vector.memset(w_plane[1][:].bitcast(I32), 0)
-        ones = keep.tile([P, P], BF16, name="ones")
-        nc.vector.memset(ones[:], 1.0)
         gain32 = keep.tile([P, H], F32, name="gain32")
+        ones = keep.tile([P, P], BF16, name="ones")
+        nc.vector.memset(gain_row[:], 0.0)
+        one = keep.tile([P, 1], F32, name="one")
+        nc.vector.memset(one[:], 1.0)
+        nc.vector.memset(w_plane[0][:].bitcast(I32), 0)
 
         load_x(0, 2)
         nc.sync.dma_start(out=gain_row[0:1, :], in_=q_gain.unsqueeze(0))
         load_w_scales(0)
         load_w(0, 1)
         load_x(1, 1)
-        load_w_scales(1)
-        load_w(1, 1)
-        load_x(2, 1)
 
         idle = psum.tile([P, 512], F32, tag="bank")
 
@@ -118,26 +115,36 @@ def tile_causalselfattention_pa_kernel(tc, x, w_words, w_scales, q_gain, out_0, 
         idle_matmuls(4)
 
         ratio = ROPE_BASE ** (-1.0 / HALF)
-        turns = keep.tile([P, 2, HALF, NT], F32, name="turns")
+        freq = keep.tile([P, HALF], F32, name="freq")
         for d in range(4):
-            nc.vector.tensor_scalar_mul(out=turns[:, 1, d, :], in0=tpos[:], scalar1=ratio ** d / TWO_PI)
+            nc.vector.tensor_scalar_mul(out=freq[:, d : d + 1], in0=one[:], scalar1=ratio ** d / TWO_PI)
+        nc.vector.memset(w_plane[1][:].bitcast(I32), 0)
         for n in (4, 16):
             for m in range(1, 4):
-                nc.vector.tensor_scalar_mul(
-                    out=turns[:, 1, n * m : n * (m + 1), :], in0=turns[:, 1, 0:n, :], scalar1=ratio ** (n * m)
-                )
-        nc.vector.tensor_scalar_add(out=turns[:, 0, :, :], in0=turns[:, 1, :, :], scalar1=0.25)
-        whole = keep.tile([P, 2, HALF, NT], I32, name="whole")
-        nc.vector.tensor_copy(out=whole[:], in_=turns[:])
-        frac = keep.tile([P, 2, HALF, NT], F32, name="frac")
-        nc.vector.tensor_tensor(out=frac[:], in0=turns[:], in1=whole[:], op=ALU.subtract)
+                nc.vector.tensor_scalar_mul(out=freq[:, n * m : n * (m + 1)], in0=freq[:, 0:n], scalar1=ratio ** (n * m))
+            if n == 4:
+                nc.vector.memset(ones[:], 1.0)
+        load_w_scales(1)
+        load_w(1, 1)
+        load_x(2, 1)
+        turns = keep.tile([P, NT, 2, HALF], F32, name="turns")
+        for a in range(NT):
+            nc.vector.tensor_scalar(out=turns[:, a, 0, :], in0=freq[:], scalar1=tpos[:, a : a + 1], scalar2=0.25, op0=ALU.mult, op1=ALU.add)
+            nc.vector.tensor_scalar(out=turns[:, a, 1, :], in0=freq[:], scalar1=tpos[:, a : a + 1], scalar2=None, op0=ALU.mult)
+        whole = keep.tile([P, NT, 2, HALF], I32, name="whole")
+        frac = keep.tile([P, NT, 2, HALF], F32, name="frac")
+        for a in range(0, NT, 2):
+            nc.vector.tensor_copy(out=whole[:, a : a + 2, :, :], in_=turns[:, a : a + 2, :, :])
+        for a in range(0, NT, 2):
+            nc.vector.tensor_tensor(
+                out=frac[:, a : a + 2, :, :], in0=turns[:, a : a + 2, :, :], in1=whole[:, a : a + 2, :, :], op=ALU.subtract
+            )
         tab = keep.tile([P, NT, 4, HALF], F32, name="tab")
 
         def scalar_tables():
-            part = frac[:].rearrange("p c d a -> p a c d")
-            nc.scalar.activation(out=tab[:, :, 0:2, :], in_=part, func=ACT.Sin, scale=TWO_PI)
-            nc.scalar.activation(out=tab[:, :, 2, :], in_=part[:, :, 1, :], func=ACT.Sin, scale=-TWO_PI)
-            nc.scalar.activation(out=tab[:, :, 3, :], in_=part[:, :, 0, :], func=ACT.Sin, scale=TWO_PI)
+            nc.scalar.activation(out=tab[:, :, 0:2, :], in_=frac[:], func=ACT.Sin, scale=TWO_PI)
+            nc.scalar.activation(out=tab[:, :, 2, :], in_=frac[:, :, 1, :], func=ACT.Sin, scale=-TWO_PI)
+            nc.scalar.activation(out=tab[:, :, 3, :], in_=frac[:, :, 0, :], func=ACT.Sin, scale=TWO_PI)
             nc.scalar.activation(out=warm[:, 1:2], in_=eps_t[:], func=ACT.Abs_reciprocal_sqrt)
             nc.scalar.copy(out=gain32[:], in_=idle[:, P : P + H])
 
@@ -318,6 +325,7 @@ def tile_causalselfattention_pa_kernel(tc, x, w_words, w_scales, q_gain, out_0, 
 
         mm(0, 0)
         flip(1)
+        idle_matmuls(3)
         copy_half(1, 0, vcopy)
         copy_half(1, 1, vcopy)
         quant(1, 0, 1)

@@ -206,76 +206,62 @@ def tile_causalselfattention_pa_kernel(tc, x, w_words, w_scales, q_gain, out_0, 
         n_rope = NT * V_GROUP
         state = {"done": 0}
 
-        def mean_squares(acc):
-            ss = small.tile([P, HPG], F32, tag="ss")
-            for h in range(HPG):
-                junk = work.tile([P, HD], F32, tag="junk")
-                nc.scalar.activation(
-                    out=junk[:], in_=acc[:, HD * h : HD * (h + 1)], func=ACT.Square,
-                    scale=HD ** -0.5, accum_out=ss[:, h : h + 1],
-                )
-            return ss
-
-        def inverse_root(ss):
-            rs = small.tile([P, HPG], F32, tag="rs")
-            nc.scalar.activation(out=rs[:], in_=ss[:], func=ACT.Abs_reciprocal_sqrt, bias=eps_t[:], scale=1.0)
-            return rs
-
-        def times_gain(j, rs):
-            if j == K_GROUP:
-                return rs
-            rg = small.tile([P, HPG], F32, tag="rg")
-            for h in range(HPG):
-                nc.scalar.activation(
-                    out=rg[:, h : h + 1], in_=rs[:, h : h + 1], func=ACT.Copy,
-                    scale=gain32[:, HPG * j + h : HPG * j + h + 1],
-                )
-            return rg
-
-        def norm_factors(a, j, acc):
-            return times_gain(j, inverse_root(mean_squares(acc)))
-
-        held = []
-
-        def rotate(a, j, acc, rg):
-            ab = work.tile([P, 2 * 512], F32, tag="ab")
-            state["done"] += 1
-            pend = {"acc": acc, "rg": rg, "a": a, "j": j, "ab": ab, "late": state["done"] > n_rope - 2}
-            for h in reversed(range(HPG)):
-                rope_head(pend, h)
-                if h == HPG - 2 and held:
-                    finish(held[0])
-                    held.clear()
-            if state["done"] == n_rope - 1:
-                held.append(pend)
-            elif state["done"] == n_rope:
-                finish(pend, 2)
-            else:
-                finish(pend)
-
-        waiting = []
-
-        def flush():
-            for a, j, acc, rs in waiting:
-                rotate(a, j, acc, times_gain(j, rs))
-            waiting.clear()
-
         acc, sums, root, factor = {}, {}, {}, {}
 
         def mm(a, j):
             acc[a, j] = mx_unit(a, j)
 
         def squares(a, j):
-            sums[a, j] = mean_squares(acc[a, j])
+            ss = small.tile([P, HPG], F32, tag="ss")
+            sums[a, j] = ss
+            for h in range(HPG):
+                junk = work.tile([P, HD], F32, tag="junk")
+                nc.scalar.activation(
+                    out=junk[:], in_=acc[a, j][:, HD * h : HD * (h + 1)], func=ACT.Square,
+                    scale=HD ** -0.5, accum_out=ss[:, h : h + 1],
+                )
 
         def roots(a, j):
-            root[a, j] = inverse_root(sums[a, j])
+            rs = small.tile([P, HPG], F32, tag="rs")
+            root[a, j] = rs
+            nc.scalar.activation(out=rs[:], in_=sums[a, j][:], func=ACT.Abs_reciprocal_sqrt, bias=eps_t[:], scale=1.0)
 
         def gains(a, j):
-            factor[a, j] = times_gain(j, root[a, j])
+            factor[a, j] = root[a, j]
+            if j < K_GROUP:
+                rg = small.tile([P, HPG], F32, tag="rg")
+                factor[a, j] = rg
+                for h in range(HPG):
+                    nc.scalar.activation(
+                        out=rg[:, h : h + 1], in_=root[a, j][:, h : h + 1], func=ACT.Copy,
+                        scale=gain32[:, HPG * j + h : HPG * j + h + 1],
+                    )
+
+        def gains_g(a, j):
+            rg = small.tile([P, HPG], F32, tag="rg")
+            factor[a, j] = rg
+            nc.gpsimd.tensor_tensor(
+                out=rg[:], in0=root[a, j][:], in1=gain32[:, HPG * j : HPG * (j + 1)], op=ALU.mult
+            )
+
+        held = []
+        on_vector = ((3, 2), (3, 3))
 
         def turn(a, j):
-            rotate(a, j, acc[a, j], factor[a, j])
+            ab = work.tile([P, 2 * 512], F32, tag="ab")
+            state["done"] += 1
+            pend = {"acc": acc[a, j], "rg": factor[a, j], "a": a, "j": j, "ab": ab, "late": state["done"] > n_rope - 2 or (a, j) in on_vector}
+            for h in reversed(range(HPG)):
+                rope_head(pend, h)
+                if h == HPG - 2 and held:
+                    finish(held[0])
+                    held.clear()
+            if state["done"] == n_rope:
+                finish(pend, 2)
+            elif pend["late"]:
+                held.append(pend)
+            else:
+                finish(pend)
 
         def plain(a, j):
             pieces = 2 if a == NT - 1 else 1
@@ -376,8 +362,21 @@ def tile_causalselfattention_pa_kernel(tc, x, w_words, w_scales, q_gain, out_0, 
         roots(2, 1)
         before = (2, 1)
         for u in [(2, 2), (3, 0), (3, 1), (3, 2)] + [(a, j) for j in range(3, NJ) for a in range(NT)]:
+            if u[0] == "q":
+                quant(u[1], 0, 1)
+                continue
+            if u[0] == "f":
+                flip(u[1])
+                continue
+            if u[0] in ("c", "C"):
+                copy_half(u[1], u[2], scopy if u[0] == "c" else vcopy)
+                continue
             mm(*u)
             if u[1] == V_GROUP:
+                if before:
+                    gains(*before)
+                    turn(*before)
+                    before = None
                 plain(*u)
                 continue
             squares(*u)
@@ -385,5 +384,3 @@ def tile_causalselfattention_pa_kernel(tc, x, w_words, w_scales, q_gain, out_0, 
             turn(*before)
             roots(*u)
             before = u
-        gains(*before)
-        turn(*before)

from contextlib import ExitStack

import concourse.mybir as mybir
from concourse.masks import make_identity

S, DIM, H, NKV, HD = 512, 2048, 16, 4, 128
HALF = HD // 2
NCOLS = (H + 2 * NKV) * HD
FLOPS = 2 * S * DIM * NCOLS
ROPE_BASE = 10000.0
RMS_EPS_F32 = 2.0 ** -23
TWO_PI = 6.283185307179586

F32 = mybir.dt.float32
BF16 = mybir.dt.bfloat16
I32 = mybir.dt.int32
U32 = mybir.dt.uint32
U8 = mybir.dt.uint8
E5M2X4 = mybir.dt.float8_e5m2_x4
E2M1X4 = mybir.dt.float4_e2m1fn_x4
ACT = mybir.ActivationFunctionType
ALU = mybir.AluOpType

P = 128
NT = S // P
NG = DIM // 512
NJ = NCOLS // 512
K_GROUP = 4
V_GROUP = 5
HPG = 4


def tile_causalselfattention_pa_kernel(tc, x, w_words, w_scales, q_gain, out_0, out_1, out_2):
    nc = tc.nc
    x2d = x.flatten_outer_dims()
    outs = [
        out_0.rearrange("b t h d -> (b t) (h d)"),
        out_1.rearrange("b t h d -> (b t) (h d)"),
        out_2.rearrange("b t h d -> (b t) (h d)"),
    ]

    with ExitStack() as ctx:
        keep = ctx.enter_context(tc.tile_pool(name="keep", bufs=1))
        small = ctx.enter_context(tc.tile_pool(name="small", bufs=6))
        work = ctx.enter_context(tc.tile_pool(name="work", bufs=6))
        outp = ctx.enter_context(tc.tile_pool(name="outp", bufs=NT * NJ + 2))
        psum = ctx.enter_context(tc.psum_pool(name="psum", bufs=8))
        ctx.enter_context(tc.manual_schedule())

        x_sb = [keep.tile([P, DIM], BF16, name="x_sb%d" % a, align_bytes=64) for a in range(NT)]
        grouped = [keep.tile([P, DIM], BF16, name="grouped%d" % a, align_bytes=64) for a in range(NT)]
        x_codes = [keep.tile([P, DIM // 4], U32, name="x_codes%d" % a, align_bytes=64) for a in range(NT)]
        x_scales = [keep.tile([P, DIM // 4], U8, name="x_scales%d" % a, align_bytes=64) for a in range(NT)]
        w_sb = [keep.tile([P, NG, 1024], U8, name="w_sb%d" % j, align_bytes=64) for j in range(NJ)]
        plane_of = [0, 1, 2, 3, 3, 3]
        first_of = [0, 1, 2, 3]
        plane_n = [1, 1, 1, 3]
        w_plane = [keep.tile([P, NG, 512 * plane_n[i]], U8, name="w_plane%d" % i, align_bytes=64) for i in range(4)]

        def load_x(a, pieces):
            width = DIM // pieces
            for c in range(pieces):
                nc.sync.dma_start(
                    out=x_sb[a][:, width * c : width * (c + 1)], in_=x2d[P * a : P * (a + 1), width * c : width * (c + 1)]
                )

        def load_w(j, pieces):
            n_g = NG // pieces
            for c in range(pieces):
                nc.sync.dma_start(
                    out=w_sb[j][:, n_g * c : n_g * (c + 1), :].bitcast(I32),
                    in_=w_words[n_g * c : n_g * (c + 1), :, 1024 * j : 1024 * (j + 1)].rearrange("g p n -> p g n").bitcast(I32),
                )

        def load_w_scales(i):
            n = 512 * plane_n[i]
            for r in range(4):
                nc.sync.dma_start(
                    out=w_plane[i][r : P : 32, :, :].bitcast(I32),
                    in_=w_scales[:, r : 16 : 4, 512 * first_of[i] : 512 * first_of[i] + n]
                    .rearrange("g q n -> q g n")
                    .bitcast(I32),
                )

        eps_t = keep.tile([P, 1], F32, name="eps_t")
        nc.vector.memset(eps_t[:], RMS_EPS_F32)
        warm = keep.tile([P, 2], F32, name="warm")
        nc.scalar.activation(out=warm[:, 0:1], in_=eps_t[:], func=ACT.Sin)

        tpos = keep.tile([P, NT], F32, name="tpos")
        nc.gpsimd.iota(tpos[:], pattern=[[P, NT]], base=0, channel_multiplier=1, allow_small_or_imprecise_dtypes=True)
        ident = keep.tile([P, P], F32, name="ident")
        make_identity(nc, ident[:])

        gain_row = keep.tile([P, H], BF16, name="gain_row")
        gain32 = keep.tile([P, H], F32, name="gain32")
        ones = keep.tile([P, P], BF16, name="ones")
        nc.vector.memset(gain_row[:], 0.0)
        one = keep.tile([P, 1], F32, name="one")
        nc.vector.memset(one[:], 1.0)
        nc.vector.memset(w_plane[0][:].bitcast(I32), 0)

        load_x(0, 2)
        nc.sync.dma_start(out=gain_row[0:1, :], in_=q_gain.unsqueeze(0))
        load_w_scales(0)
        load_w(0, 1)
        load_x(1, 1)

        idle = psum.tile([P, 512], F32, tag="bank")

        def idle_matmuls(n):
            for i in range(n):
                nc.tensor.matmul(idle[:, 0:P], lhsT=ident[:], rhs=ident[:], start=True, stop=True)

        idle_matmuls(4)

        ratio = ROPE_BASE ** (-1.0 / HALF)
        freq = keep.tile([P, HALF], F32, name="freq")
        for d in range(4):
            nc.vector.tensor_scalar_mul(out=freq[:, d : d + 1], in0=one[:], scalar1=ratio ** d / TWO_PI)
        nc.vector.memset(w_plane[1][:].bitcast(I32), 0)
        for n in (4, 16):
            for m in range(1, 4):
                nc.vector.tensor_scalar_mul(out=freq[:, n * m : n * (m + 1)], in0=freq[:, 0:n], scalar1=ratio ** (n * m))
            if n == 4:
                nc.vector.memset(ones[:], 1.0)
        load_w_scales(1)
        load_w(1, 1)
        load_x(2, 1)
        turns = keep.tile([P, NT, 2, HALF], F32, name="turns")
        for a in range(NT):
            nc.vector.tensor_scalar(out=turns[:, a, 0, :], in0=freq[:], scalar1=tpos[:, a : a + 1], scalar2=0.25, op0=ALU.mult, op1=ALU.add)
            nc.vector.tensor_scalar(out=turns[:, a, 1, :], in0=freq[:], scalar1=tpos[:, a : a + 1], scalar2=None, op0=ALU.mult)
        whole = keep.tile([P, NT, 2, HALF], I32, name="whole")
        frac = keep.tile([P, NT, 2, HALF], F32, name="frac")
        for a in range(0, NT, 2):
            nc.vector.tensor_copy(out=whole[:, a : a + 2, :, :], in_=turns[:, a : a + 2, :, :])
        for a in range(0, NT, 2):
            nc.vector.tensor_tensor(
                out=frac[:, a : a + 2, :, :], in0=turns[:, a : a + 2, :, :], in1=whole[:, a : a + 2, :, :], op=ALU.subtract
            )
        tab = keep.tile([P, NT, 4, HALF], F32, name="tab")

        def scalar_tables():
            nc.scalar.activation(out=tab[:, :, 0:2, :], in_=frac[:], func=ACT.Sin, scale=TWO_PI)
            nc.scalar.activation(out=tab[:, :, 2, :], in_=frac[:, :, 1, :], func=ACT.Sin, scale=-TWO_PI)
            nc.scalar.activation(out=tab[:, :, 3, :], in_=frac[:, :, 0, :], func=ACT.Sin, scale=TWO_PI)
            nc.scalar.activation(out=warm[:, 1:2], in_=eps_t[:], func=ACT.Abs_reciprocal_sqrt)
            nc.scalar.copy(out=gain32[:], in_=idle[:, P : P + H])

        def transpose_x(a):
            words = x_sb[a][:].bitcast(F32)
            banks = []
            for b in range(2):
                xt = psum.tile([P, 512], F32, tag="bank")
                for gg in range(2):
                    g = 2 * b + gg
                    for u in range(2):
                        nc.tensor.transpose(
                            xt[:, (2 * gg + u) * P : (2 * gg + u + 1) * P],
                            words[:, 256 * g + u : 256 * (g + 1) : 2],
                            ident[:],
                        )
                banks.append(xt)
            return banks

        def mx_unit(a, j):
            acc = psum.tile([P, 512], F32, tag="bank")
            for g in range(NG):
                nc.tensor.matmul_mx(
                    out=acc[:],
                    lhsT=x_codes[a][:, P * g : P * (g + 1)].bitcast(E5M2X4),
                    lhsT_scale=x_scales[a][:, P * g : P * (g + 1)],
                    rhs=w_sb[j][:, g, :].bitcast(E2M1X4),
                    rhs_scale=w_plane[plane_of[j]][:, g, 512 * (j - first_of[plane_of[j]]) : 512 * (j - first_of[plane_of[j]] + 1)],
                    start=(g == 0),
                    stop=(g == NG - 1),
                )
            return acc

        def rope_head(pend, h):
            nc.vector.scalar_tensor_tensor(
                out=pend["ab"][:, 2 * HD * h : 2 * HD * (h + 1)].rearrange("p (r d) -> p r d", r=2),
                in0=pend["acc"][:, HD * h : HD * (h + 1)].unsqueeze(1).to_broadcast([P, 2, HD]),
                scalar=pend["rg"][:, h : h + 1],
                in1=tab[:, pend["a"], :, :].rearrange("p (r c) d -> p r (c d)", r=2),
                op0=ALU.mult,
                op1=ALU.mult,
            )

        def finish(pend, pieces=1):
            pairs = pend["ab"][:].rearrange("p (m two d) -> p m two d", two=2, d=HALF)
            adder = nc.vector if pend["late"] else nc.gpsimd
            which, col = (0, 512 * pend["j"]) if pend["j"] < K_GROUP else (1, 0)
            w = 512 // pieces
            for c in reversed(range(pieces)):
                o = outp.tile([P, w], F32, tag="o")
                m0, m1 = (w // HALF) * c, (w // HALF) * (c + 1)
                adder.tensor_tensor(
                    out=o[:].rearrange("p (m d) -> p m d", d=HALF), in0=pairs[:, m0:m1, 0, :], in1=pairs[:, m0:m1, 1, :], op=ALU.add
                )
                nc.sync.dma_start(
                    out=outs[which][P * pend["a"] : P * (pend["a"] + 1), col + w * c : col + w * (c + 1)], in_=o[:]
                )

        n_rope = NT * V_GROUP
        state = {"done": 0}

        acc, sums, root, factor = {}, {}, {}, {}

        def mm(a, j):
            acc[a, j] = mx_unit(a, j)

        def squares(a, j):
            ss = small.tile([P, HPG], F32, tag="ss")
            sums[a, j] = ss
            for h in range(HPG):
                junk = work.tile([P, HD], F32, tag="junk")
                nc.scalar.activation(
                    out=junk[:], in_=acc[a, j][:, HD * h : HD * (h + 1)], func=ACT.Square,
                    scale=HD ** -0.5, accum_out=ss[:, h : h + 1],
                )

        def roots(a, j):
            rs = small.tile([P, HPG], F32, tag="rs")
            root[a, j] = rs
            nc.scalar.activation(out=rs[:], in_=sums[a, j][:], func=ACT.Abs_reciprocal_sqrt, bias=eps_t[:], scale=1.0)

        def gains(a, j):
            factor[a, j] = root[a, j]
            if j < K_GROUP:
                rg = small.tile([P, HPG], F32, tag="rg")
                factor[a, j] = rg
                for h in range(HPG):
                    nc.scalar.activation(
                        out=rg[:, h : h + 1], in_=root[a, j][:, h : h + 1], func=ACT.Copy,
                        scale=gain32[:, HPG * j + h : HPG * j + h + 1],
                    )

        def gains_g(a, j):
            rg = small.tile([P, HPG], F32, tag="rg")
            factor[a, j] = rg
            nc.gpsimd.tensor_tensor(
                out=rg[:], in0=root[a, j][:], in1=gain32[:, HPG * j : HPG * (j + 1)], op=ALU.mult
            )

        held = []
        on_vector = ((3, 2), (3, 3))

        def turn(a, j):
            ab = work.tile([P, 2 * 512], F32, tag="ab")
            state["done"] += 1
            pend = {"acc": acc[a, j], "rg": factor[a, j], "a": a, "j": j, "ab": ab, "late": state["done"] > n_rope - 2 or (a, j) in on_vector}
            for h in reversed(range(HPG)):
                rope_head(pend, h)
                if h == HPG - 2 and held:
                    finish(held[0])
                    held.clear()
            if state["done"] == n_rope:
                finish(pend, 2)
            elif pend["late"]:
                held.append(pend)
            else:
                finish(pend)

        def plain(a, j):
            pieces = 2 if a == NT - 1 else 1
            w = 512 // pieces
            for c in range(pieces):
                o = outp.tile([P, w], F32, tag="o")
                nc.scalar.copy(out=o[:], in_=acc[a, j][:, w * c : w * (c + 1)])
                nc.scalar.dma_start(out=outs[2][P * a : P * (a + 1), w * c : w * (c + 1)], in_=o[:])

        xt = {}

        def flip(a):
            xt[a] = transpose_x(a)

        def copy_half(a, b, engine_copy):
            engine_copy(
                out=grouped[a][:, 1024 * b : 1024 * (b + 1)].bitcast(F32).rearrange("p (g r u) -> p g r u", g=2, u=2),
                in_=xt[a][b][:].rearrange("p (g u r) -> p g r u", g=2, u=2),
            )

        def quant(a, c, pieces):
            w = DIM // pieces
            nc.vector.quantize_mx(
                out=x_codes[a][:, (w // 4) * c : (w // 4) * (c + 1)].bitcast(E5M2X4),
                scales=x_scales[a][:, (w // 4) * c : (w // 4) * (c + 1)],
                in_=grouped[a][:, w * c : w * (c + 1)],
            )

        vcopy, scopy = nc.vector.tensor_copy, nc.scalar.copy
        flip(0)
        idle_matmuls(2)
        nc.tensor.matmul(idle[:, P : P + H], lhsT=ones[:], rhs=gain_row[:], start=True, stop=True)
        copy_half(0, 0, vcopy)
        copy_half(0, 1, vcopy)
        quant(0, 0, 2)
        quant(0, 1, 2)
        scalar_tables()
        nc.vector.memset(w_plane[2][:].bitcast(I32), 0)
        nc.vector.memset(w_plane[3][:].bitcast(I32), 0)
        load_w_scales(2)
        load_w(2, 1)
        load_x(3, 1)
        load_w_scales(3)
        load_w(3, 1)
        load_w(4, 1)
        load_w(5, 1)

        mm(0, 0)
        flip(1)
        idle_matmuls(3)
        copy_half(1, 0, vcopy)
        copy_half(1, 1, vcopy)
        quant(1, 0, 1)
        squares(0, 0)
        roots(0, 0)
        gains(0, 0)
        turn(0, 0)
        mm(0, 1)
        squares(0, 1)
        roots(0, 1)
        gains(0, 1)
        turn(0, 1)
        mm(1, 0)
        squares(1, 0)
        roots(1, 0)
        mm(1, 1)
        squares(1, 1)
        gains(1, 0)
        turn(1, 0)
        roots(1, 1)
        flip(2)
        copy_half(2, 0, scopy)
        copy_half(2, 1, scopy)
        mm(0, 2)
        squares(0, 2)
        gains(1, 1)
        quant(2, 0, 1)
        turn(1, 1)
        roots(0, 2)
        mm(1, 2)
        squares(1, 2)
        gains(0, 2)
        turn(0, 2)
        roots(1, 2)
        mm(2, 0)
        flip(3)
        squares(2, 0)
        gains(1, 2)
        turn(1, 2)
        roots(2, 0)
        copy_half(3, 0, scopy)
        copy_half(3, 1, scopy)
        mm(2, 1)
        squares(2, 1)
        gains(2, 0)
        quant(3, 0, 1)
        turn(2, 0)
        roots(2, 1)
        before = (2, 1)
        for u in [(2, 2), (3, 0), (3, 1), (3, 2)] + [(a, j) for j in range(3, NJ) for a in range(NT)]:
            if u[0] == "q":
                quant(u[1], 0, 1)
                continue
            if u[0] == "f":
                flip(u[1])
                continue
            if u[0] in ("c", "C"):
                copy_half(u[1], u[2], scopy if u[0] == "c" else vcopy)
                continue
            mm(*u)
            if u[1] == V_GROUP:
                if before:
                    gains(*before)
                    turn(*before)
                    before = None
                plain(*u)
                continue
            squares(*u)
            gains(*before)
            turn(*before)
            roots(*u)
            before = u
